import numpy as np
import ml_dtypes


def mxq(x, axis, fmt="e4m3"):
    dtype, down = {"e4m3": (ml_dtypes.float8_e4m3fn, 7), "e5m2": (ml_dtypes.float8_e5m2, 14)}[fmt]
    v = np.moveaxis(np.asarray(x, np.float32).astype(ml_dtypes.bfloat16).astype(np.float64), axis, -1)
    blocks = v.reshape(v.shape[:-1] + (-1, 32))
    amax = np.abs(blocks).max(-1, keepdims=True)
    byte = np.maximum(np.where(amax > 0, np.frexp(amax)[1] - 1 + 127, 0) - down, 1)
    scale = np.exp2(byte - 127.0)
    codes = (blocks / scale).astype(np.float32).astype(dtype).astype(np.float64)
    return np.moveaxis((codes * scale).reshape(v.shape), -1, axis)


WIDE = False


def mx_kscale(k):
    if not WIDE:
        return np.ones(k)
    levels = np.array([10, -10, 5, -5, 0])
    a = np.random.permutation(np.resize(levels, k // 512 * 4)).reshape(k // 512, 4)
    idx = np.arange(k)
    return np.exp2(a[idx // 512, idx % 128 // 32])


BF16 = ml_dtypes.bfloat16


def bf(x):
    return np.asarray(x, np.float32).astype(BF16)


def f64(x):
    return np.asarray(x).astype(np.float64)


B, N, DIM, H, D, QB = 4, 2048, 1024, 2, 64, 512
E = H * D
RMS_EPS = 1e-12


def setup_inputs():
    s = mx_kscale(DIM)
    return {"x": bf(np.random.standard_normal((B, N, DIM))),
            "gamma": bf((1.0 + 0.1 * np.random.standard_normal(DIM)) * s),
            "w_qkv": bf(np.random.standard_normal((DIM, 3 * E)) * 1.5 / np.sqrt(DIM) / s[:, None])}


def reference(x, gamma, w_qkv):
    xf = f64(x)
    l2 = np.maximum(np.sqrt((xf * xf).sum(-1, keepdims=True)), RMS_EPS)
    normed = xf / l2 * np.sqrt(DIM) * f64(gamma)
    y = mxq(normed, 2, "e4m3") @ mxq(f64(w_qkv), 0, "e4m3")
    qkv = y.reshape(B, N, 3, H, D).transpose(2, 0, 3, 1, 4)
    return qkv[0] * D ** -0.5, qkv[1], qkv[2]

@@ -1,0 +1,184 @@
+from contextlib import ExitStack
+
+import concourse.mybir as mybir
+from concourse.masks import make_identity
+
+F32 = mybir.dt.float32
+BF16 = mybir.dt.bfloat16
+U32 = mybir.dt.uint32
+U8 = mybir.dt.uint8
+FP8X4 = mybir.dt.float8_e4m3fn_x4
+ALU = mybir.AluOpType
+ACT = mybir.ActivationFunctionType
+
+P = 128
+PACK = 4
+K_PASS = P * PACK
+
+BATCH, SEQ, DIM, HEADS, HEAD_DIM = 4, 2048, 1024, 2, 64
+EMB = HEADS * HEAD_DIM
+COLS = 3 * EMB
+PASSES = DIM // K_PASS
+RMS_EPS = 1e-12
+
+TILES_PER_LOAD = 4
+ROWS_PER_LOAD = P * TILES_PER_LOAD
+LOADS_PER_BATCH = SEQ // ROWS_PER_LOAD
+
+COLUMN_GROUPS = ((EMB, COLS), (0, EMB))
+
+FLOPS = 2 * BATCH * SEQ * DIM * COLS
+
+
+def quantise_weights(nc, setup, keep, w_qkv):
+    w_raw = setup.tile([P, PASSES, PACK, COLS], BF16)
+    nc.sync.dma_start(
+        out=w_raw[:], in_=w_qkv.rearrange("(g t p) n -> p g t n", t=PACK, p=P)
+    )
+    w_grouped = setup.tile([P, PASSES, COLS, PACK], BF16, align_bytes=64)
+    w_codes = keep.tile([P, PASSES, COLS], U32, align_bytes=64)
+    w_scales = keep.tile([P, PASSES, COLS], U8, align_bytes=64)
+    for g in range(PASSES):
+        nc.vector.tensor_copy(
+            out=w_grouped[:, g], in_=w_raw[:, g].rearrange("p t n -> p n t")
+        )
+    for g in range(PASSES):
+        for lo, hi in COLUMN_GROUPS:
+            nc.vector.quantize_mx(
+                out=w_codes[:, g, lo:hi].bitcast(FP8X4),
+                scales=w_scales[:, g, lo:hi],
+                in_=w_grouped[:, g, lo:hi, :].rearrange("p n t -> p (n t)"),
+            )
+    return w_codes, w_scales
+
+
+def gamma_by_partition(nc, setup, keep, psum_t, identity, gamma):
+    rows_bf16 = setup.tile([P, P], BF16)
+    nc.vector.memset(rows_bf16[:], 0.0)
+    nc.sync.dma_start(
+        out=rows_bf16[0 : PASSES * PACK, :], in_=gamma.rearrange("(r p) -> r p", p=P)
+    )
+    rows_f32 = setup.tile([P, P], F32)
+    nc.vector.tensor_copy(out=rows_f32[:], in_=rows_bf16[:])
+    turned = psum_t.tile([P, PACK, P], F32, tag="turned")
+    nc.tensor.transpose(out=turned[:, 0, :], in_=rows_f32[:], identity=identity[:])
+    gain = keep.tile([P, PASSES * PACK], F32)
+    nc.vector.tensor_copy(out=gain[:], in_=turned[:, 0, 0 : PASSES * PACK])
+    return gain
+
+
+def tile_ringattention_pa_t_kernel(tc, x, gamma, w_qkv, out_0, out_1, out_2):
+    nc = tc.nc
+    x_loads = x.rearrange(
+        "b (c p s) k -> (b c) p s k", p=P, s=TILES_PER_LOAD
+    )
+    out_views = [
+        o.rearrange("b h (c p s) d -> b c p h s d", p=P, s=TILES_PER_LOAD)
+        for o in (out_0, out_1, out_2)
+    ]
+
+    with ExitStack() as ctx:
+        setup = ctx.enter_context(tc.tile_pool(name="setup", bufs=1))
+        keep = ctx.enter_context(tc.tile_pool(name="keep", bufs=1))
+        x_pool = ctx.enter_context(tc.tile_pool(name="x", bufs=3))
+        stat_pool = ctx.enter_context(tc.tile_pool(name="stat", bufs=3))
+        square_pool = ctx.enter_context(tc.tile_pool(name="square", bufs=2))
+        scaled_pool = ctx.enter_context(tc.tile_pool(name="scaled", bufs=4))
+        mx_pool = ctx.enter_context(tc.tile_pool(name="mx", bufs=4))
+        y_pool = ctx.enter_context(tc.tile_pool(name="y", bufs=3))
+        psum_t = ctx.enter_context(tc.psum_pool(name="psum_t", bufs=4))
+        psum_y = ctx.enter_context(tc.psum_pool(name="psum_y", bufs=3))
+
+        one = setup.tile([P, 1], F32)
+        nc.vector.memset(one[:], 1.0)
+        nc.scalar.sqrt(out=one[:], in_=one[:])
+
+        identity = keep.tile([P, P], F32)
+        make_identity(nc, identity[:])
+        gain = gamma_by_partition(nc, setup, keep, psum_t, identity, gamma)
+        w_codes, w_scales = quantise_weights(nc, setup, keep, w_qkv)
+
+        for load in range(BATCH * LOADS_PER_BATCH):
+            b, c = divmod(load, LOADS_PER_BATCH)
+            x_sb = x_pool.tile([P, TILES_PER_LOAD, DIM], BF16)
+            nc.sync.dma_start(out=x_sb[:], in_=x_loads[load])
+
+            sum_sq = stat_pool.tile([P, TILES_PER_LOAD], F32)
+            for s in range(TILES_PER_LOAD):
+                squares = square_pool.tile([P, DIM], BF16)
+                nc.scalar.activation(
+                    out=squares[:],
+                    in_=x_sb[:, s, :],
+                    func=ACT.Square,
+                    accum_out=sum_sq[:, s : s + 1],
+                )
+            l2_over_32 = stat_pool.tile([P, TILES_PER_LOAD], F32)
+            nc.vector.tensor_scalar_max(out=l2_over_32[:], in0=sum_sq[:], scalar1=RMS_EPS**2)
+            nc.scalar.activation(
+                out=l2_over_32[:], in_=l2_over_32[:], func=ACT.Sqrt, scale=1.0 / DIM
+            )
+            row_scale = stat_pool.tile([P, TILES_PER_LOAD], F32)
+            nc.vector.reciprocal(out=row_scale[:], in_=l2_over_32[:])
+
+            y_sb = y_pool.tile([P, 3, HEADS, TILES_PER_LOAD, HEAD_DIM], F32)
+            for s in range(TILES_PER_LOAD):
+                scaled = scaled_pool.tile([P, DIM], F32)
+                nc.gpsimd.tensor_scalar(
+                    out=scaled[:],
+                    in0=x_sb[:, s, :],
+                    scalar1=row_scale[:, s : s + 1],
+                    scalar2=0.0,
+                    op0=ALU.mult,
+                    op1=ALU.add,
+                )
+
+                grouped = mx_pool.tile([P, PASSES, P, PACK], BF16, align_bytes=64)
+                for g in range(PASSES):
+                    turned = psum_t.tile([P, PACK, P], F32, tag="turned")
+                    for t in range(PACK):
+                        k0 = g * K_PASS + t * P
+                        nc.tensor.transpose(
+                            out=turned[:, t, :], in_=scaled[:, k0 : k0 + P], identity=identity[:]
+                        )
+                    nc.vector.tensor_tensor(
+                        out=grouped[:, g],
+                        in0=turned[:].rearrange("p t i -> p i t"),
+                        in1=gain[:, g * PACK : (g + 1) * PACK]
+                        .unsqueeze(1)
+                        .to_broadcast([P, P, PACK]),
+                        op=ALU.mult,
+                    )
+
+                codes = mx_pool.tile([P, PASSES, P], U32, align_bytes=64)
+                scales = mx_pool.tile([P, PASSES, P], U8, align_bytes=64)
+                nc.vector.quantize_mx(
+                    out=codes[:].rearrange("p g i -> p (g i)").bitcast(FP8X4),
+                    scales=scales[:].rearrange("p g i -> p (g i)"),
+                    in_=grouped[:].rearrange("p g i t -> p (g i t)"),
+                )
+
+                y_ps = psum_y.tile([P, COLS], F32)
+                for lo, hi in COLUMN_GROUPS:
+                    for g in range(PASSES):
+                        nc.tensor.matmul_mx(
+                            out=y_ps[:, lo:hi],
+                            lhsT=codes[:, g, :].bitcast(FP8X4),
+                            lhsT_scale=scales[:, g, :],
+                            rhs=w_codes[:, g, lo:hi].bitcast(FP8X4),
+                            rhs_scale=w_scales[:, g, lo:hi],
+                            start=(g == 0),
+                            stop=(g == PASSES - 1),
+                        )
+
+                nc.scalar.mul(
+                    out=y_sb[:, 0, :, s, :],
+                    in_=y_ps[:, 0:EMB].rearrange("p (h d) -> p h d", h=HEADS),
+                    mul=HEAD_DIM**-0.5,
+                )
+                nc.scalar.copy(
+                    out=y_sb[:, 1:3, :, s, :],
+                    in_=y_ps[:, EMB:COLS].rearrange("p (j h d) -> p j h d", j=2, h=HEADS),
+                )
+
+            for j in range(3):
+                nc.sync.dma_start(out=out_views[j][b, c], in_=y_sb[:, j])

@@ -25,7 +25,7 @@ TILES_PER_LOAD = 4
 ROWS_PER_LOAD = P * TILES_PER_LOAD
 LOADS_PER_BATCH = SEQ // ROWS_PER_LOAD
 
-COLUMN_GROUPS = ((EMB, COLS), (0, EMB))
+MOVING_COLS = 512
 
 FLOPS = 2 * BATCH * SEQ * DIM * COLS
 
@@ -35,20 +35,20 @@ def quantise_weights(nc, setup, keep, w_qkv):
     nc.sync.dma_start(
         out=w_raw[:], in_=w_qkv.rearrange("(g t p) n -> p g t n", t=PACK, p=P)
     )
-    w_grouped = setup.tile([P, PASSES, COLS, PACK], BF16, align_bytes=64)
-    w_codes = keep.tile([P, PASSES, COLS], U32, align_bytes=64)
-    w_scales = keep.tile([P, PASSES, COLS], U8, align_bytes=64)
+    w_grouped = setup.tile([P, PASSES, MOVING_COLS, PACK], BF16, align_bytes=64)
+    w_codes = keep.tile([P, PASSES, MOVING_COLS], U32, align_bytes=64)
+    w_scales = keep.tile([P, PASSES, MOVING_COLS], U8, align_bytes=64)
+    nc.vector.memset(w_grouped[:, :, COLS:MOVING_COLS, :], 0.0)
     for g in range(PASSES):
         nc.vector.tensor_copy(
-            out=w_grouped[:, g], in_=w_raw[:, g].rearrange("p t n -> p n t")
+            out=w_grouped[:, g, 0:COLS, :], in_=w_raw[:, g].rearrange("p t n -> p n t")
         )
     for g in range(PASSES):
-        for lo, hi in COLUMN_GROUPS:
-            nc.vector.quantize_mx(
-                out=w_codes[:, g, lo:hi].bitcast(FP8X4),
-                scales=w_scales[:, g, lo:hi],
-                in_=w_grouped[:, g, lo:hi, :].rearrange("p n t -> p (n t)"),
-            )
+        nc.vector.quantize_mx(
+            out=w_codes[:, g, :].bitcast(FP8X4),
+            scales=w_scales[:, g, :],
+            in_=w_grouped[:, g].rearrange("p n t -> p (n t)"),
+        )
     return w_codes, w_scales
 
 
@@ -157,18 +157,17 @@ def tile_ringattention_pa_t_kernel(tc, x, gamma, w_qkv, out_0, out_1, out_2):
                     in_=grouped[:].rearrange("p g i t -> p (g i t)"),
                 )
 
-                y_ps = psum_y.tile([P, COLS], F32)
-                for lo, hi in COLUMN_GROUPS:
-                    for g in range(PASSES):
-                        nc.tensor.matmul_mx(
-                            out=y_ps[:, lo:hi],
-                            lhsT=codes[:, g, :].bitcast(FP8X4),
-                            lhsT_scale=scales[:, g, :],
-                            rhs=w_codes[:, g, lo:hi].bitcast(FP8X4),
-                            rhs_scale=w_scales[:, g, lo:hi],
-                            start=(g == 0),
-                            stop=(g == PASSES - 1),
-                        )
+                y_ps = psum_y.tile([P, MOVING_COLS], F32)
+                for g in range(PASSES):
+                    nc.tensor.matmul_mx(
+                        out=y_ps[:],
+                        lhsT=codes[:, g, :].bitcast(FP8X4),
+                        lhsT_scale=scales[:, g, :],
+                        rhs=w_codes[:, g, :].bitcast(FP8X4),
+                        rhs_scale=w_scales[:, g, :],
+                        start=(g == 0),
+                        stop=(g == PASSES - 1),
+                    )
 
                 nc.scalar.mul(
                     out=y_sb[:, 0, :, s, :],

@@ -13,6 +13,7 @@ ACT = mybir.ActivationFunctionType
 
 P = 128
 PACK = 4
+PAIR = 2
 K_PASS = P * PACK
 
 BATCH, SEQ, DIM, HEADS, HEAD_DIM = 4, 2048, 1024, 2, 64
@@ -20,21 +21,18 @@ EMB = HEADS * HEAD_DIM
 COLS = 3 * EMB
 PASSES = DIM // K_PASS
 RMS_EPS = 1e-12
+N_TILES = BATCH * SEQ // P
 
-TILES_PER_LOAD = 4
-ROWS_PER_LOAD = P * TILES_PER_LOAD
-LOADS_PER_BATCH = SEQ // ROWS_PER_LOAD
+TILES_PER_STORE = 4
+TILES_PER_LOAD = 2
+STORES_PER_BATCH = SEQ // (P * TILES_PER_STORE)
 
 MOVING_COLS = 512
 
 FLOPS = 2 * BATCH * SEQ * DIM * COLS
 
 
-def quantise_weights(nc, setup, keep, w_qkv):
-    w_raw = setup.tile([P, PASSES, PACK, COLS], BF16)
-    nc.sync.dma_start(
-        out=w_raw[:], in_=w_qkv.rearrange("(g t p) n -> p g t n", t=PACK, p=P)
-    )
+def quantise_weights(nc, setup, keep, w_raw):
     w_grouped = setup.tile([P, PASSES, MOVING_COLS, PACK], BF16, align_bytes=64)
     w_codes = keep.tile([P, PASSES, MOVING_COLS], U32, align_bytes=64)
     w_scales = keep.tile([P, PASSES, MOVING_COLS], U8, align_bytes=64)
@@ -52,132 +50,172 @@ def quantise_weights(nc, setup, keep, w_qkv):
     return w_codes, w_scales
 
 
-def gamma_by_partition(nc, setup, keep, psum_t, identity, gamma):
-    rows_bf16 = setup.tile([P, P], BF16)
-    nc.vector.memset(rows_bf16[:], 0.0)
-    nc.sync.dma_start(
-        out=rows_bf16[0 : PASSES * PACK, :], in_=gamma.rearrange("(r p) -> r p", p=P)
-    )
-    rows_f32 = setup.tile([P, P], F32)
-    nc.vector.tensor_copy(out=rows_f32[:], in_=rows_bf16[:])
-    turned = psum_t.tile([P, PACK, P], F32, tag="turned")
-    nc.tensor.transpose(out=turned[:, 0, :], in_=rows_f32[:], identity=identity[:])
-    gain = keep.tile([P, PASSES * PACK], F32)
-    nc.vector.tensor_copy(out=gain[:], in_=turned[:, 0, 0 : PASSES * PACK])
-    return gain
+SCALE_LAG = 3
+TURN_LAG = SCALE_LAG + 1
+REGROUP_LAG = TURN_LAG + 1
+QUANTISE_LAG = REGROUP_LAG + 1
+PROJECT_LAG = QUANTISE_LAG + 1
+EMIT_LAG = PROJECT_LAG + 1
+STORE_LAG = EMIT_LAG + 1
+LOADS_AHEAD = 3
 
 
 def tile_ringattention_pa_t_kernel(tc, x, gamma, w_qkv, out_0, out_1, out_2):
     nc = tc.nc
-    x_loads = x.rearrange(
-        "b (c p s) k -> (b c) p s k", p=P, s=TILES_PER_LOAD
-    )
+    x_groups = x.rearrange("b (c p s) k -> (b c) p s k", p=P, s=TILES_PER_STORE)
     out_views = [
-        o.rearrange("b h (c p s) d -> b c p h s d", p=P, s=TILES_PER_LOAD)
+        o.rearrange("b h (c p s) d -> b c p h s d", p=P, s=TILES_PER_STORE)
         for o in (out_0, out_1, out_2)
     ]
+    n_loads = N_TILES // TILES_PER_LOAD
 
     with ExitStack() as ctx:
+        ctx.enter_context(tc.manual_schedule())
         setup = ctx.enter_context(tc.tile_pool(name="setup", bufs=1))
         keep = ctx.enter_context(tc.tile_pool(name="keep", bufs=1))
-        x_pool = ctx.enter_context(tc.tile_pool(name="x", bufs=3))
-        stat_pool = ctx.enter_context(tc.tile_pool(name="stat", bufs=3))
+        x_pool = ctx.enter_context(tc.tile_pool(name="x", bufs=2 * LOADS_AHEAD))
+        stat_pool = ctx.enter_context(tc.tile_pool(name="stat", bufs=4))
         square_pool = ctx.enter_context(tc.tile_pool(name="square", bufs=2))
-        scaled_pool = ctx.enter_context(tc.tile_pool(name="scaled", bufs=4))
-        mx_pool = ctx.enter_context(tc.tile_pool(name="mx", bufs=4))
+        work = ctx.enter_context(tc.tile_pool(name="work", bufs=3))
         y_pool = ctx.enter_context(tc.tile_pool(name="y", bufs=3))
-        psum_t = ctx.enter_context(tc.psum_pool(name="psum_t", bufs=4))
+        psum_t = ctx.enter_context(tc.psum_pool(name="psum_t", bufs=3))
         psum_y = ctx.enter_context(tc.psum_pool(name="psum_y", bufs=3))
 
-        one = setup.tile([P, 1], F32)
-        nc.vector.memset(one[:], 1.0)
-        nc.scalar.sqrt(out=one[:], in_=one[:])
+        x_sb, sum_sq, row_scale = {}, {}, {}
+        normed, turned, grouped, codes, scales, y_ps, y_sb = {}, {}, {}, {}, {}, {}, {}
 
+        def load_rows(h):
+            group, half = divmod(h, TILES_PER_STORE // TILES_PER_LOAD)
+            x_sb[h] = x_pool.tile([P, TILES_PER_LOAD, DIM], BF16, name="x_sb")
+            s0 = half * TILES_PER_LOAD
+            nc.sync.dma_start(out=x_sb[h][:], in_=x_groups[group][:, s0 : s0 + TILES_PER_LOAD, :])
+
+        def sum_squares(j):
+            h, s = divmod(j, TILES_PER_LOAD)
+            if s == 0:
+                sum_sq[h] = stat_pool.tile([P, TILES_PER_LOAD], F32, name="sum_sq")
+            squares = square_pool.tile([P, DIM], BF16)
+            nc.scalar.activation(
+                out=squares[:],
+                in_=x_sb[h][:, s, :],
+                func=ACT.Square,
+                accum_out=sum_sq[h][:, s : s + 1],
+            )
+            if s == TILES_PER_LOAD - 1:
+                unclamped = stat_pool.tile([P, TILES_PER_LOAD], F32)
+                nc.scalar.activation(
+                    out=unclamped[:],
+                    in_=sum_sq[h][:],
+                    func=ACT.Abs_reciprocal_sqrt,
+                    scale=1.0 / DIM,
+                )
+                row_scale[h] = stat_pool.tile([P, TILES_PER_LOAD], F32, name="row_scale")
+                nc.gpsimd.tensor_scalar_min(
+                    out=row_scale[h][:], in0=unclamped[:], scalar1=DIM**0.5 / RMS_EPS
+                )
+
+        def scale_rows(j):
+            h, s = divmod(j, TILES_PER_LOAD)
+            normed[j] = work.tile([P, DIM], BF16, name="normed")
+            nc.vector.scalar_tensor_tensor(
+                out=normed[j][:],
+                in0=x_sb[h][:, s, :],
+                scalar=row_scale[h][:, s : s + 1],
+                in1=gamma_all[:],
+                op0=ALU.mult,
+                op1=ALU.mult,
+            )
+
+        def turn(j):
+            words = normed[j][:].bitcast(F32)
+            turned[j] = psum_t.tile([P, PASSES, PAIR, P], F32, name="turned")
+            for g in range(PASSES):
+                for u in range(PAIR):
+                    w0 = (g * PAIR + u) * P
+                    nc.tensor.transpose(
+                        out=turned[j][:, g, u, :], in_=words[:, w0 : w0 + P], identity=identity[:]
+                    )
+
+        def regroup(j):
+            grouped[j] = work.tile([P, PASSES, P, PAIR], F32, name="grouped", align_bytes=64)
+            nc.scalar.copy(out=grouped[j][:], in_=turned[j][:].rearrange("p g u i -> p g i u"))
+
+        def quantise(j):
+            codes[j] = work.tile([P, PASSES, P], U32, name="codes", align_bytes=64)
+            scales[j] = work.tile([P, PASSES, P], U8, name="scales", align_bytes=64)
+            nc.vector.quantize_mx(
+                out=codes[j][:].rearrange("p g i -> p (g i)").bitcast(FP8X4),
+                scales=scales[j][:].rearrange("p g i -> p (g i)"),
+                in_=grouped[j][:].rearrange("p g i u -> p (g i u)").bitcast(BF16),
+            )
+
+        def project(j):
+            y_ps[j] = psum_y.tile([P, MOVING_COLS], F32, name="y_ps")
+            for g in range(PASSES):
+                nc.tensor.matmul_mx(
+                    out=y_ps[j][:],
+                    lhsT=codes[j][:, g, :].bitcast(FP8X4),
+                    lhsT_scale=scales[j][:, g, :],
+                    rhs=w_codes[:, g, :].bitcast(FP8X4),
+                    rhs_scale=w_scales[:, g, :],
+                    start=(g == 0),
+                    stop=(g == PASSES - 1),
+                )
+
+        def emit(j):
+            group, s = divmod(j, TILES_PER_STORE)
+            if s == 0:
+                y_sb[group] = y_pool.tile(
+                    [P, 3, HEADS, TILES_PER_STORE, HEAD_DIM], F32, name="y_sb"
+                )
+            nc.vector.tensor_scalar_mul(
+                out=y_sb[group][:, 0, :, s, :],
+                in0=y_ps[j][:, 0:EMB].rearrange("p (h d) -> p h d", h=HEADS),
+                scalar1=HEAD_DIM**-0.5,
+            )
+            nc.vector.tensor_copy(
+                out=y_sb[group][:, 1:3, :, s, :],
+                in_=y_ps[j][:, EMB:COLS].rearrange("p (j h d) -> p j h d", j=2, h=HEADS),
+            )
+
+        def store(group):
+            b, c = divmod(group, STORES_PER_BATCH)
+            for tensor in range(3):
+                nc.sync.dma_start(out=out_views[tensor][b, c], in_=y_sb[group][:, tensor])
+
+        w_raw = setup.tile([P, PASSES, PACK, COLS], BF16)
+        nc.sync.dma_start(
+            out=w_raw[:].rearrange("p g (u e) n -> p (g u) (e n)", e=PAIR),
+            in_=w_qkv.rearrange("(a p e) n -> p a (e n)", p=P, e=PAIR),
+        )
+        load_rows(0)
+        gamma_all = keep.tile([P, DIM], BF16)
+        nc.sync.dma_start(out=gamma_all[:], in_=gamma.partition_broadcast(P))
+        for h in range(1, LOADS_AHEAD):
+            load_rows(h)
         identity = keep.tile([P, P], F32)
         make_identity(nc, identity[:])
-        gain = gamma_by_partition(nc, setup, keep, psum_t, identity, gamma)
-        w_codes, w_scales = quantise_weights(nc, setup, keep, w_qkv)
+        w_codes, w_scales = quantise_weights(nc, setup, keep, w_raw)
 
-        for load in range(BATCH * LOADS_PER_BATCH):
-            b, c = divmod(load, LOADS_PER_BATCH)
-            x_sb = x_pool.tile([P, TILES_PER_LOAD, DIM], BF16)
-            nc.sync.dma_start(out=x_sb[:], in_=x_loads[load])
+        def due(j):
+            return 0 <= j < N_TILES
 
-            sum_sq = stat_pool.tile([P, TILES_PER_LOAD], F32)
-            for s in range(TILES_PER_LOAD):
-                squares = square_pool.tile([P, DIM], BF16)
-                nc.scalar.activation(
-                    out=squares[:],
-                    in_=x_sb[:, s, :],
-                    func=ACT.Square,
-                    accum_out=sum_sq[:, s : s + 1],
-                )
-            l2_over_32 = stat_pool.tile([P, TILES_PER_LOAD], F32)
-            nc.vector.tensor_scalar_max(out=l2_over_32[:], in0=sum_sq[:], scalar1=RMS_EPS**2)
-            nc.scalar.activation(
-                out=l2_over_32[:], in_=l2_over_32[:], func=ACT.Sqrt, scale=1.0 / DIM
-            )
-            row_scale = stat_pool.tile([P, TILES_PER_LOAD], F32)
-            nc.vector.reciprocal(out=row_scale[:], in_=l2_over_32[:])
-
-            y_sb = y_pool.tile([P, 3, HEADS, TILES_PER_LOAD, HEAD_DIM], F32)
-            for s in range(TILES_PER_LOAD):
-                scaled = scaled_pool.tile([P, DIM], F32)
-                nc.gpsimd.tensor_scalar(
-                    out=scaled[:],
-                    in0=x_sb[:, s, :],
-                    scalar1=row_scale[:, s : s + 1],
-                    scalar2=0.0,
-                    op0=ALU.mult,
-                    op1=ALU.add,
-                )
-
-                grouped = mx_pool.tile([P, PASSES, P, PACK], BF16, align_bytes=64)
-                for g in range(PASSES):
-                    turned = psum_t.tile([P, PACK, P], F32, tag="turned")
-                    for t in range(PACK):
-                        k0 = g * K_PASS + t * P
-                        nc.tensor.transpose(
-                            out=turned[:, t, :], in_=scaled[:, k0 : k0 + P], identity=identity[:]
-                        )
-                    nc.vector.tensor_tensor(
-                        out=grouped[:, g],
-                        in0=turned[:].rearrange("p t i -> p i t"),
-                        in1=gain[:, g * PACK : (g + 1) * PACK]
-                        .unsqueeze(1)
-                        .to_broadcast([P, P, PACK]),
-                        op=ALU.mult,
-                    )
-
-                codes = mx_pool.tile([P, PASSES, P], U32, align_bytes=64)
-                scales = mx_pool.tile([P, PASSES, P], U8, align_bytes=64)
-                nc.vector.quantize_mx(
-                    out=codes[:].rearrange("p g i -> p (g i)").bitcast(FP8X4),
-                    scales=scales[:].rearrange("p g i -> p (g i)"),
-                    in_=grouped[:].rearrange("p g i t -> p (g i t)"),
-                )
-
-                y_ps = psum_y.tile([P, MOVING_COLS], F32)
-                for g in range(PASSES):
-                    nc.tensor.matmul_mx(
-                        out=y_ps[:],
-                        lhsT=codes[:, g, :].bitcast(FP8X4),
-                        lhsT_scale=scales[:, g, :],
-                        rhs=w_codes[:, g, :].bitcast(FP8X4),
-                        rhs_scale=w_scales[:, g, :],
-                        start=(g == 0),
-                        stop=(g == PASSES - 1),
-                    )
-
-                nc.scalar.mul(
-                    out=y_sb[:, 0, :, s, :],
-                    in_=y_ps[:, 0:EMB].rearrange("p (h d) -> p h d", h=HEADS),
-                    mul=HEAD_DIM**-0.5,
-                )
-                nc.scalar.copy(
-                    out=y_sb[:, 1:3, :, s, :],
-                    in_=y_ps[:, EMB:COLS].rearrange("p (j h d) -> p j h d", j=2, h=HEADS),
-                )
-
-            for j in range(3):
-                nc.sync.dma_start(out=out_views[j][b, c], in_=y_sb[:, j])
+        for step in range(N_TILES + STORE_LAG):
+            if step % TILES_PER_LOAD == 0 and step // TILES_PER_LOAD + LOADS_AHEAD < n_loads:
+                load_rows(step // TILES_PER_LOAD + LOADS_AHEAD)
+            if due(step - STORE_LAG) and (step - STORE_LAG) % TILES_PER_STORE == TILES_PER_STORE - 1:
+                store((step - STORE_LAG) // TILES_PER_STORE)
+            if due(step - EMIT_LAG):
+                emit(step - EMIT_LAG)
+            if due(step - PROJECT_LAG):
+                project(step - PROJECT_LAG)
+            if due(step - QUANTISE_LAG):
+                quantise(step - QUANTISE_LAG)
+            if due(step - REGROUP_LAG):
+                regroup(step - REGROUP_LAG)
+            if due(step - TURN_LAG):
+                turn(step - TURN_LAG)
+            if due(step - SCALE_LAG):
+                scale_rows(step - SCALE_LAG)
+            if due(step):
+                sum_squares(step)

@@ -168,15 +168,19 @@ def tile_ringattention_pa_t_kernel(tc, x, gamma, w_qkv, out_0, out_1, out_2):
                 y_sb[group] = y_pool.tile(
                     [P, 3, HEADS, TILES_PER_STORE, HEAD_DIM], F32, name="y_sb"
                 )
-            nc.vector.tensor_scalar_mul(
-                out=y_sb[group][:, 0, :, s, :],
-                in0=y_ps[j][:, 0:EMB].rearrange("p (h d) -> p h d", h=HEADS),
-                scalar1=HEAD_DIM**-0.5,
-            )
-            nc.vector.tensor_copy(
-                out=y_sb[group][:, 1:3, :, s, :],
-                in_=y_ps[j][:, EMB:COLS].rearrange("p (j h d) -> p j h d", j=2, h=HEADS),
-            )
+            scalar_is_free = j >= N_TILES - EMIT_LAG
+            q_ps = y_ps[j][:, 0:EMB].rearrange("p (h d) -> p h d", h=HEADS)
+            q_sb = y_sb[group][:, 0, :, s, :]
+            kv_ps = y_ps[j][:, EMB:COLS].rearrange("p (j h d) -> p j h d", j=2, h=HEADS)
+            kv_sb = y_sb[group][:, 1:3, :, s, :]
+            if scalar_is_free or j % 2 == 1:
+                nc.scalar.mul(out=q_sb, in_=q_ps, mul=HEAD_DIM**-0.5)
+            else:
+                nc.vector.tensor_scalar_mul(out=q_sb, in0=q_ps, scalar1=HEAD_DIM**-0.5)
+            if scalar_is_free:
+                nc.scalar.copy(out=kv_sb, in_=kv_ps)
+            else:
+                nc.vector.tensor_copy(out=kv_sb, in_=kv_ps)
 
         def store(group):
             b, c = divmod(group, STORES_PER_BATCH)
@@ -184,14 +188,13 @@ def tile_ringattention_pa_t_kernel(tc, x, gamma, w_qkv, out_0, out_1, out_2):
                 nc.sync.dma_start(out=out_views[tensor][b, c], in_=y_sb[group][:, tensor])
 
         w_raw = setup.tile([P, PASSES, PACK, COLS], BF16)
-        nc.sync.dma_start(
+        nc.scalar.dma_start(
             out=w_raw[:].rearrange("p g (u e) n -> p (g u) (e n)", e=PAIR),
             in_=w_qkv.rearrange("(a p e) n -> p a (e n)", p=P, e=PAIR),
         )
-        load_rows(0)
         gamma_all = keep.tile([P, DIM], BF16)
-        nc.sync.dma_start(out=gamma_all[:], in_=gamma.partition_broadcast(P))
-        for h in range(1, LOADS_AHEAD):
+        nc.scalar.dma_start(out=gamma_all[:], in_=gamma.partition_broadcast(P))
+        for h in range(LOADS_AHEAD):
             load_rows(h)
         identity = keep.tile([P, P], F32)
         make_identity(nc, identity[:])

@@ -13,7 +13,6 @@ ACT = mybir.ActivationFunctionType
 
 P = 128
 PACK = 4
-PAIR = 2
 K_PASS = P * PACK
 
 BATCH, SEQ, DIM, HEADS, HEAD_DIM = 4, 2048, 1024, 2, 64
@@ -50,11 +49,26 @@ def quantise_weights(nc, setup, keep, w_raw):
     return w_codes, w_scales
 
 
+def gamma_by_partition(nc, setup, keep, psum_t, identity, gamma):
+    rows_bf16 = setup.tile([P, P], BF16)
+    nc.vector.memset(rows_bf16[:], 0.0)
+    nc.scalar.dma_start(
+        out=rows_bf16[0 : PASSES * PACK, :], in_=gamma.rearrange("(r p) -> r p", p=P)
+    )
+    rows_f32 = setup.tile([P, P], F32)
+    nc.vector.tensor_copy(out=rows_f32[:], in_=rows_bf16[:])
+    gamma_ps = psum_t.tile([P, PACK, P], F32, tag="turned")
+    nc.tensor.transpose(out=gamma_ps[:, 0, :], in_=rows_f32[:], identity=identity[:])
+    gain = keep.tile([P, PASSES * PACK], F32)
+    nc.vector.tensor_copy(out=gain[:], in_=gamma_ps[:, 0, 0 : PASSES * PACK])
+    return gain
+
+
 SCALE_LAG = 3
 TURN_LAG = SCALE_LAG + 1
-REGROUP_LAG = TURN_LAG + 1
-QUANTISE_LAG = REGROUP_LAG + 1
-PROJECT_LAG = QUANTISE_LAG + 1
+GAIN_LAG = TURN_LAG + 1
+QUANTISE_LAG = GAIN_LAG + 1
+PROJECT_LAG = QUANTISE_LAG + TILES_PER_STORE
 EMIT_LAG = PROJECT_LAG + 1
 STORE_LAG = EMIT_LAG + 1
 LOADS_AHEAD = 3
@@ -76,13 +90,14 @@ def tile_ringattention_pa_t_kernel(tc, x, gamma, w_qkv, out_0, out_1, out_2):
         x_pool = ctx.enter_context(tc.tile_pool(name="x", bufs=2 * LOADS_AHEAD))
         stat_pool = ctx.enter_context(tc.tile_pool(name="stat", bufs=4))
         square_pool = ctx.enter_context(tc.tile_pool(name="square", bufs=2))
-        work = ctx.enter_context(tc.tile_pool(name="work", bufs=3))
+        scaled_pool = ctx.enter_context(tc.tile_pool(name="scaled", bufs=3))
+        mx_pool = ctx.enter_context(tc.tile_pool(name="mx", bufs=3))
         y_pool = ctx.enter_context(tc.tile_pool(name="y", bufs=3))
-        psum_t = ctx.enter_context(tc.psum_pool(name="psum_t", bufs=3))
+        psum_t = ctx.enter_context(tc.psum_pool(name="psum_t", bufs=5))
         psum_y = ctx.enter_context(tc.psum_pool(name="psum_y", bufs=3))
 
         x_sb, sum_sq, row_scale = {}, {}, {}
-        normed, turned, grouped, codes, scales, y_ps, y_sb = {}, {}, {}, {}, {}, {}, {}
+        scaled, turned, grouped, codes, scales, y_ps, y_sb = {}, {}, {}, {}, {}, {}, {}
 
         def load_rows(h):
             group, half = divmod(h, TILES_PER_STORE // TILES_PER_LOAD)
@@ -116,46 +131,62 @@ def tile_ringattention_pa_t_kernel(tc, x, gamma, w_qkv, out_0, out_1, out_2):
 
         def scale_rows(j):
             h, s = divmod(j, TILES_PER_LOAD)
-            normed[j] = work.tile([P, DIM], BF16, name="normed")
-            nc.vector.scalar_tensor_tensor(
-                out=normed[j][:],
+            scaled[j] = scaled_pool.tile([P, DIM], F32, name="scaled")
+            nc.gpsimd.tensor_scalar(
+                out=scaled[j][:],
                 in0=x_sb[h][:, s, :],
-                scalar=row_scale[h][:, s : s + 1],
-                in1=gamma_all[:],
+                scalar1=row_scale[h][:, s : s + 1],
+                scalar2=0.0,
                 op0=ALU.mult,
-                op1=ALU.mult,
+                op1=ALU.add,
             )
 
         def turn(j):
-            words = normed[j][:].bitcast(F32)
-            turned[j] = psum_t.tile([P, PASSES, PAIR, P], F32, name="turned")
             for g in range(PASSES):
-                for u in range(PAIR):
-                    w0 = (g * PAIR + u) * P
+                turned[j, g] = psum_t.tile([P, PACK, P], F32, name="turned")
+                for t in range(PACK):
+                    k0 = g * K_PASS + t * P
                     nc.tensor.transpose(
-                        out=turned[j][:, g, u, :], in_=words[:, w0 : w0 + P], identity=identity[:]
+                        out=turned[j, g][:, t, :],
+                        in_=scaled[j][:, k0 : k0 + P],
+                        identity=identity[:],
                     )
 
-        def regroup(j):
-            grouped[j] = work.tile([P, PASSES, P, PAIR], F32, name="grouped", align_bytes=64)
-            nc.scalar.copy(out=grouped[j][:], in_=turned[j][:].rearrange("p g u i -> p g i u"))
+        def apply_gain(j):
+            group, s = divmod(j, TILES_PER_STORE)
+            if s == 0:
+                grouped[group] = mx_pool.tile(
+                    [P, TILES_PER_STORE, PASSES, P, PACK], BF16, name="grouped", align_bytes=64
+                )
+            for g in range(PASSES):
+                nc.vector.tensor_tensor(
+                    out=grouped[group][:, s, g],
+                    in0=turned[j, g][:].rearrange("p t i -> p i t"),
+                    in1=gain[:, g * PACK : (g + 1) * PACK].unsqueeze(1).to_broadcast([P, P, PACK]),
+                    op=ALU.mult,
+                )
 
-        def quantise(j):
-            codes[j] = work.tile([P, PASSES, P], U32, name="codes", align_bytes=64)
-            scales[j] = work.tile([P, PASSES, P], U8, name="scales", align_bytes=64)
+        def quantise(group):
+            codes[group] = mx_pool.tile(
+                [P, TILES_PER_STORE, PASSES, P], U32, name="codes", align_bytes=64
+            )
+            scales[group] = mx_pool.tile(
+                [P, TILES_PER_STORE, PASSES, P], U8, name="scales", align_bytes=64
+            )
             nc.vector.quantize_mx(
-                out=codes[j][:].rearrange("p g i -> p (g i)").bitcast(FP8X4),
-                scales=scales[j][:].rearrange("p g i -> p (g i)"),
-                in_=grouped[j][:].rearrange("p g i u -> p (g i u)").bitcast(BF16),
+                out=codes[group][:].rearrange("p s g i -> p (s g i)").bitcast(FP8X4),
+                scales=scales[group][:].rearrange("p s g i -> p (s g i)"),
+                in_=grouped[group][:].rearrange("p s g i t -> p (s g i t)"),
             )
 
         def project(j):
+            group, s = divmod(j, TILES_PER_STORE)
             y_ps[j] = psum_y.tile([P, MOVING_COLS], F32, name="y_ps")
             for g in range(PASSES):
                 nc.tensor.matmul_mx(
                     out=y_ps[j][:],
-                    lhsT=codes[j][:, g, :].bitcast(FP8X4),
-                    lhsT_scale=scales[j][:, g, :],
+                    lhsT=codes[group][:, s, g, :].bitcast(FP8X4),
+                    lhsT_scale=scales[group][:, s, g, :],
                     rhs=w_codes[:, g, :].bitcast(FP8X4),
                     rhs_scale=w_scales[:, g, :],
                     start=(g == 0),
@@ -171,16 +202,14 @@ def tile_ringattention_pa_t_kernel(tc, x, gamma, w_qkv, out_0, out_1, out_2):
             scalar_is_free = j >= N_TILES - EMIT_LAG
             q_ps = y_ps[j][:, 0:EMB].rearrange("p (h d) -> p h d", h=HEADS)
             q_sb = y_sb[group][:, 0, :, s, :]
-            kv_ps = y_ps[j][:, EMB:COLS].rearrange("p (j h d) -> p j h d", j=2, h=HEADS)
-            kv_sb = y_sb[group][:, 1:3, :, s, :]
-            if scalar_is_free or j % 2 == 1:
+            if scalar_is_free or j % 2 == 0:
                 nc.scalar.mul(out=q_sb, in_=q_ps, mul=HEAD_DIM**-0.5)
             else:
                 nc.vector.tensor_scalar_mul(out=q_sb, in0=q_ps, scalar1=HEAD_DIM**-0.5)
-            if scalar_is_free:
-                nc.scalar.copy(out=kv_sb, in_=kv_ps)
-            else:
-                nc.vector.tensor_copy(out=kv_sb, in_=kv_ps)
+            nc.scalar.copy(
+                out=y_sb[group][:, 1:3, :, s, :],
+                in_=y_ps[j][:, EMB:COLS].rearrange("p (j h d) -> p j h d", j=2, h=HEADS),
+            )
 
         def store(group):
             b, c = divmod(group, STORES_PER_BATCH)
@@ -189,33 +218,34 @@ def tile_ringattention_pa_t_kernel(tc, x, gamma, w_qkv, out_0, out_1, out_2):
 
         w_raw = setup.tile([P, PASSES, PACK, COLS], BF16)
         nc.scalar.dma_start(
-            out=w_raw[:].rearrange("p g (u e) n -> p (g u) (e n)", e=PAIR),
-            in_=w_qkv.rearrange("(a p e) n -> p a (e n)", p=P, e=PAIR),
+            out=w_raw[:], in_=w_qkv.rearrange("(g t p) n -> p g t n", t=PACK, p=P)
         )
-        gamma_all = keep.tile([P, DIM], BF16)
-        nc.scalar.dma_start(out=gamma_all[:], in_=gamma.partition_broadcast(P))
         for h in range(LOADS_AHEAD):
             load_rows(h)
         identity = keep.tile([P, P], F32)
         make_identity(nc, identity[:])
+        gain = gamma_by_partition(nc, setup, keep, psum_t, identity, gamma)
         w_codes, w_scales = quantise_weights(nc, setup, keep, w_raw)
 
         def due(j):
             return 0 <= j < N_TILES
 
+        def ends_group(j):
+            return due(j) and j % TILES_PER_STORE == TILES_PER_STORE - 1
+
         for step in range(N_TILES + STORE_LAG):
             if step % TILES_PER_LOAD == 0 and step // TILES_PER_LOAD + LOADS_AHEAD < n_loads:
                 load_rows(step // TILES_PER_LOAD + LOADS_AHEAD)
-            if due(step - STORE_LAG) and (step - STORE_LAG) % TILES_PER_STORE == TILES_PER_STORE - 1:
+            if ends_group(step - STORE_LAG):
                 store((step - STORE_LAG) // TILES_PER_STORE)
             if due(step - EMIT_LAG):
                 emit(step - EMIT_LAG)
             if due(step - PROJECT_LAG):
                 project(step - PROJECT_LAG)
-            if due(step - QUANTISE_LAG):
-                quantise(step - QUANTISE_LAG)
-            if due(step - REGROUP_LAG):
-                regroup(step - REGROUP_LAG)
+            if ends_group(step - QUANTISE_LAG):
+                quantise((step - QUANTISE_LAG) // TILES_PER_STORE)
+            if due(step - GAIN_LAG):
+                apply_gain(step - GAIN_LAG)
             if due(step - TURN_LAG):
                 turn(step - TURN_LAG)
             if due(step - SCALE_LAG):

from contextlib import ExitStack

import concourse.mybir as mybir
from concourse.masks import make_identity

F32 = mybir.dt.float32
BF16 = mybir.dt.bfloat16
U32 = mybir.dt.uint32
U8 = mybir.dt.uint8
FP8X4 = mybir.dt.float8_e4m3fn_x4
ALU = mybir.AluOpType
ACT = mybir.ActivationFunctionType

P = 128
PACK = 4
K_PASS = P * PACK

BATCH, SEQ, DIM, HEADS, HEAD_DIM = 4, 2048, 1024, 2, 64
EMB = HEADS * HEAD_DIM
COLS = 3 * EMB
PASSES = DIM // K_PASS
RMS_EPS = 1e-12
N_TILES = BATCH * SEQ // P

TILES_PER_STORE = 4
TILES_PER_LOAD = 2
STORES_PER_BATCH = SEQ // (P * TILES_PER_STORE)

MOVING_COLS = 512

FLOPS = 2 * BATCH * SEQ * DIM * COLS


def quantise_weights(nc, setup, keep, w_raw):
    w_grouped = setup.tile([P, PASSES, MOVING_COLS, PACK], BF16, align_bytes=64)
    w_codes = keep.tile([P, PASSES, MOVING_COLS], U32, align_bytes=64)
    w_scales = keep.tile([P, PASSES, MOVING_COLS], U8, align_bytes=64)
    nc.vector.memset(w_grouped[:, :, COLS:MOVING_COLS, :], 0.0)
    for g in range(PASSES):
        nc.vector.tensor_copy(
            out=w_grouped[:, g, 0:COLS, :], in_=w_raw[:, g].rearrange("p t n -> p n t")
        )
    for g in range(PASSES):
        nc.vector.quantize_mx(
            out=w_codes[:, g, :].bitcast(FP8X4),
            scales=w_scales[:, g, :],
            in_=w_grouped[:, g].rearrange("p n t -> p (n t)"),
        )
    return w_codes, w_scales


def gamma_by_partition(nc, setup, keep, psum_t, identity, gamma):
    rows_bf16 = setup.tile([P, P], BF16)
    nc.vector.memset(rows_bf16[:], 0.0)
    nc.scalar.dma_start(
        out=rows_bf16[0 : PASSES * PACK, :], in_=gamma.rearrange("(r p) -> r p", p=P)
    )
    rows_f32 = setup.tile([P, P], F32)
    nc.vector.tensor_copy(out=rows_f32[:], in_=rows_bf16[:])
    gamma_ps = psum_t.tile([P, PACK, P], F32, tag="turned")
    nc.tensor.transpose(out=gamma_ps[:, 0, :], in_=rows_f32[:], identity=identity[:])
    gain = keep.tile([P, PASSES * PACK], F32)
    nc.vector.tensor_copy(out=gain[:], in_=gamma_ps[:, 0, 0 : PASSES * PACK])
    return gain


SCALE_LAG = 3
TURN_LAG = SCALE_LAG + 1
GAIN_LAG = TURN_LAG + 1
QUANTISE_LAG = GAIN_LAG + 1
PROJECT_LAG = QUANTISE_LAG + TILES_PER_STORE
EMIT_LAG = PROJECT_LAG + 1
STORE_LAG = EMIT_LAG + 1
LOADS_AHEAD = 3


def tile_ringattention_pa_t_kernel(tc, x, gamma, w_qkv, out_0, out_1, out_2):
    nc = tc.nc
    x_groups = x.rearrange("b (c p s) k -> (b c) p s k", p=P, s=TILES_PER_STORE)
    out_views = [
        o.rearrange("b h (c p s) d -> b c p h s d", p=P, s=TILES_PER_STORE)
        for o in (out_0, out_1, out_2)
    ]
    n_loads = N_TILES // TILES_PER_LOAD

    with ExitStack() as ctx:
        ctx.enter_context(tc.manual_schedule())
        setup = ctx.enter_context(tc.tile_pool(name="setup", bufs=1))
        keep = ctx.enter_context(tc.tile_pool(name="keep", bufs=1))
        x_pool = ctx.enter_context(tc.tile_pool(name="x", bufs=2 * LOADS_AHEAD))
        stat_pool = ctx.enter_context(tc.tile_pool(name="stat", bufs=4))
        square_pool = ctx.enter_context(tc.tile_pool(name="square", bufs=2))
        scaled_pool = ctx.enter_context(tc.tile_pool(name="scaled", bufs=3))
        mx_pool = ctx.enter_context(tc.tile_pool(name="mx", bufs=3))
        y_pool = ctx.enter_context(tc.tile_pool(name="y", bufs=3))
        psum_t = ctx.enter_context(tc.psum_pool(name="psum_t", bufs=5))
        psum_y = ctx.enter_context(tc.psum_pool(name="psum_y", bufs=3))

        x_sb, sum_sq, row_scale = {}, {}, {}
        scaled, turned, grouped, codes, scales, y_ps, y_sb = {}, {}, {}, {}, {}, {}, {}

        def load_rows(h):
            group, half = divmod(h, TILES_PER_STORE // TILES_PER_LOAD)
            x_sb[h] = x_pool.tile([P, TILES_PER_LOAD, DIM], BF16, name="x_sb")
            s0 = half * TILES_PER_LOAD
            nc.sync.dma_start(out=x_sb[h][:], in_=x_groups[group][:, s0 : s0 + TILES_PER_LOAD, :])

        def sum_squares(j):
            h, s = divmod(j, TILES_PER_LOAD)
            if s == 0:
                sum_sq[h] = stat_pool.tile([P, TILES_PER_LOAD], F32, name="sum_sq")
            squares = square_pool.tile([P, DIM], BF16)
            nc.scalar.activation(
                out=squares[:],
                in_=x_sb[h][:, s, :],
                func=ACT.Square,
                accum_out=sum_sq[h][:, s : s + 1],
            )
            if s == TILES_PER_LOAD - 1:
                unclamped = stat_pool.tile([P, TILES_PER_LOAD], F32)
                nc.scalar.activation(
                    out=unclamped[:],
                    in_=sum_sq[h][:],
                    func=ACT.Abs_reciprocal_sqrt,
                    scale=1.0 / DIM,
                )
                row_scale[h] = stat_pool.tile([P, TILES_PER_LOAD], F32, name="row_scale")
                nc.gpsimd.tensor_scalar_min(
                    out=row_scale[h][:], in0=unclamped[:], scalar1=DIM**0.5 / RMS_EPS
                )

        def scale_rows(j):
            h, s = divmod(j, TILES_PER_LOAD)
            scaled[j] = scaled_pool.tile([P, DIM], F32, name="scaled")
            nc.gpsimd.tensor_scalar(
                out=scaled[j][:],
                in0=x_sb[h][:, s, :],
                scalar1=row_scale[h][:, s : s + 1],
                scalar2=0.0,
                op0=ALU.mult,
                op1=ALU.add,
            )

        def turn(j):
            for g in range(PASSES):
                turned[j, g] = psum_t.tile([P, PACK, P], F32, name="turned")
                for t in range(PACK):
                    k0 = g * K_PASS + t * P
                    nc.tensor.transpose(
                        out=turned[j, g][:, t, :],
                        in_=scaled[j][:, k0 : k0 + P],
                        identity=identity[:],
                    )

        def apply_gain(j):
            group, s = divmod(j, TILES_PER_STORE)
            if s == 0:
                grouped[group] = mx_pool.tile(
                    [P, TILES_PER_STORE, PASSES, P, PACK], BF16, name="grouped", align_bytes=64
                )
            for g in range(PASSES):
                nc.vector.tensor_tensor(
                    out=grouped[group][:, s, g],
                    in0=turned[j, g][:].rearrange("p t i -> p i t"),
                    in1=gain[:, g * PACK : (g + 1) * PACK].unsqueeze(1).to_broadcast([P, P, PACK]),
                    op=ALU.mult,
                )

        def quantise(group):
            codes[group] = mx_pool.tile(
                [P, TILES_PER_STORE, PASSES, P], U32, name="codes", align_bytes=64
            )
            scales[group] = mx_pool.tile(
                [P, TILES_PER_STORE, PASSES, P], U8, name="scales", align_bytes=64
            )
            nc.vector.quantize_mx(
                out=codes[group][:].rearrange("p s g i -> p (s g i)").bitcast(FP8X4),
                scales=scales[group][:].rearrange("p s g i -> p (s g i)"),
                in_=grouped[group][:].rearrange("p s g i t -> p (s g i t)"),
            )

        def project(j):
            group, s = divmod(j, TILES_PER_STORE)
            y_ps[j] = psum_y.tile([P, MOVING_COLS], F32, name="y_ps")
            for g in range(PASSES):
                nc.tensor.matmul_mx(
                    out=y_ps[j][:],
                    lhsT=codes[group][:, s, g, :].bitcast(FP8X4),
                    lhsT_scale=scales[group][:, s, g, :],
                    rhs=w_codes[:, g, :].bitcast(FP8X4),
                    rhs_scale=w_scales[:, g, :],
                    start=(g == 0),
                    stop=(g == PASSES - 1),
                )

        def emit(j):
            group, s = divmod(j, TILES_PER_STORE)
            if s == 0:
                y_sb[group] = y_pool.tile(
                    [P, 3, HEADS, TILES_PER_STORE, HEAD_DIM], F32, name="y_sb"
                )
            scalar_is_free = j >= N_TILES - EMIT_LAG
            q_ps = y_ps[j][:, 0:EMB].rearrange("p (h d) -> p h d", h=HEADS)
            q_sb = y_sb[group][:, 0, :, s, :]
            if scalar_is_free or j % 2 == 0:
                nc.scalar.mul(out=q_sb, in_=q_ps, mul=HEAD_DIM**-0.5)
            else:
                nc.vector.tensor_scalar_mul(out=q_sb, in0=q_ps, scalar1=HEAD_DIM**-0.5)
            nc.scalar.copy(
                out=y_sb[group][:, 1:3, :, s, :],
                in_=y_ps[j][:, EMB:COLS].rearrange("p (j h d) -> p j h d", j=2, h=HEADS),
            )

        def store(group):
            b, c = divmod(group, STORES_PER_BATCH)
            for tensor in range(3):
                nc.sync.dma_start(out=out_views[tensor][b, c], in_=y_sb[group][:, tensor])

        w_raw = setup.tile([P, PASSES, PACK, COLS], BF16)
        nc.scalar.dma_start(
            out=w_raw[:], in_=w_qkv.rearrange("(g t p) n -> p g t n", t=PACK, p=P)
        )
        for h in range(LOADS_AHEAD):
            load_rows(h)
        identity = keep.tile([P, P], F32)
        make_identity(nc, identity[:])
        gain = gamma_by_partition(nc, setup, keep, psum_t, identity, gamma)
        w_codes, w_scales = quantise_weights(nc, setup, keep, w_raw)

        def due(j):
            return 0 <= j < N_TILES

        def ends_group(j):
            return due(j) and j % TILES_PER_STORE == TILES_PER_STORE - 1

        for step in range(N_TILES + STORE_LAG):
            if step % TILES_PER_LOAD == 0 and step // TILES_PER_LOAD + LOADS_AHEAD < n_loads:
                load_rows(step // TILES_PER_LOAD + LOADS_AHEAD)
            if ends_group(step - STORE_LAG):
                store((step - STORE_LAG) // TILES_PER_STORE)
            if due(step - EMIT_LAG):
                emit(step - EMIT_LAG)
            if due(step - PROJECT_LAG):
                project(step - PROJECT_LAG)
            if ends_group(step - QUANTISE_LAG):
                quantise((step - QUANTISE_LAG) // TILES_PER_STORE)
            if due(step - GAIN_LAG):
                apply_gain(step - GAIN_LAG)
            if due(step - TURN_LAG):
                turn(step - TURN_LAG)
            if due(step - SCALE_LAG):
                scale_rows(step - SCALE_LAG)
            if due(step):
                sum_squares(step)
